import numpy as np
import ml_dtypes


def mxq(x, axis, fmt="e4m3"):
    dtype, down = {"e4m3": (ml_dtypes.float8_e4m3fn, 7), "e5m2": (ml_dtypes.float8_e5m2, 14)}[fmt]
    v = np.moveaxis(np.asarray(x, np.float32).astype(ml_dtypes.bfloat16).astype(np.float64), axis, -1)
    blocks = v.reshape(v.shape[:-1] + (-1, 32))
    amax = np.abs(blocks).max(-1, keepdims=True)
    byte = np.maximum(np.where(amax > 0, np.frexp(amax)[1] - 1 + 127, 0) - down, 1)
    scale = np.exp2(byte - 127.0)
    codes = (blocks / scale).astype(np.float32).astype(dtype).astype(np.float64)
    return np.moveaxis((codes * scale).reshape(v.shape), -1, axis)


WIDE = False


def mx_kscale(k):
    if not WIDE:
        return np.ones(k)
    levels = np.array([10, -10, 5, -5, 0])
    a = np.random.permutation(np.resize(levels, k // 512 * 4)).reshape(k // 512, 4)
    idx = np.arange(k)
    return np.exp2(a[idx // 512, idx % 128 // 32])


BF16 = ml_dtypes.bfloat16


def bf(x):
    return np.asarray(x, np.float32).astype(BF16)


def f64(x):
    return np.asarray(x).astype(np.float64)


B, S, E, H, D = 4, 512, 1024, 8, 64
TD = 2 * D
K = H * TD
DEPTH = 12
LAMBDA_INIT = 0.8 - 0.6 * np.exp(-0.3 * DEPTH)
EPS = 1e-8
LS = 0.55 / D ** 0.25


def setup_inputs():
    t = mx_kscale(K)[:TD]
    tk = np.tile(t, H)
    return {'attn1': bf(np.random.standard_normal((B, S, H, TD)) * 0.7),
            'attn2': bf(np.random.standard_normal((B, S, H, TD)) * 0.7),
            'lambda_q1': bf(np.random.standard_normal(D) * LS),
            'lambda_k1': bf(np.random.standard_normal(D) * LS),
            'lambda_q2': bf(np.random.standard_normal(D) * LS),
            'lambda_k2': bf(np.random.standard_normal(D) * LS),
            'ln_w': bf((1.0 + 0.1 * np.random.standard_normal(TD)) * t),
            'ln_b': bf(0.1 * np.random.standard_normal(TD) * t),
            'Wo': bf(np.random.standard_normal((K, E)) * 2.0 / np.sqrt(K) / tk[:, None])}


def reference(attn1, attn2, lambda_q1, lambda_k1, lambda_q2, lambda_k2, ln_w, ln_b, Wo):
    lam = (np.exp(np.sum(f64(lambda_q1) * f64(lambda_k1)))
           - np.exp(np.sum(f64(lambda_q2) * f64(lambda_k2))) + LAMBDA_INIT)
    a = f64(attn1) - lam * f64(attn2)
    rms = 1.0 / np.sqrt(np.mean(a * a, axis=-1, keepdims=True) + EPS)
    a = a * rms * f64(ln_w) + f64(ln_b)
    a = a * (1.0 - LAMBDA_INIT)
    h = a.reshape(B, S, K)
    return mxq(h, 2, 'e4m3') @ mxq(f64(Wo), 0, 'e4m3')

@@ -1,0 +1,259 @@
+import math
+from contextlib import ExitStack
+
+import concourse.mybir as mybir
+from concourse.masks import make_identity
+
+F32 = mybir.dt.float32
+BF16 = mybir.dt.bfloat16
+U32 = mybir.dt.uint32
+U8 = mybir.dt.uint8
+FP8X4 = mybir.dt.float8_e4m3fn_x4
+ALU = mybir.AluOpType
+ACT = mybir.ActivationFunctionType
+AX = mybir.AxisListType
+
+P = 128
+TOKENS = 4 * 512
+HEADS = 8
+TD = 128
+K = HEADS * TD
+E = 1024
+LAM_D = 64
+PACK = 4
+K_PASS = P * PACK
+PASSES = K // K_PASS
+HEADS_PER_PASS = K_PASS // TD
+N_COLS = 512
+N_BANKS = E // N_COLS
+TILES = TOKENS // P
+WO_PIECES = 8
+PIECES_PER_PASS = WO_PIECES // PASSES
+PIECE_COLS = E // PIECES_PER_PASS
+PROJECTIONS_A_STEP = TILES // (TILES - WO_PIECES)
+LAMBDA_INIT = 0.8 - 0.6 * math.exp(-0.3 * 12)
+EPS = 1e-8
+
+FLOPS = 2 * TOKENS * K * E
+
+
+def tile_multiheadflashdiff_pb_kernel(
+    tc, attn1, attn2, lambda_q1, lambda_k1, lambda_q2, lambda_k2, ln_w, ln_b, Wo, out
+):
+    nc = tc.nc
+    with ExitStack() as ctx:
+        consts = ctx.enter_context(tc.tile_pool(name="consts", bufs=1))
+        resident = ctx.enter_context(tc.tile_pool(name="resident", bufs=1))
+        wo_stage = ctx.enter_context(tc.tile_pool(name="wo_stage", bufs=2))
+        diff_pool = ctx.enter_context(tc.tile_pool(name="diff_pool", bufs=5))
+        square_pool = ctx.enter_context(tc.tile_pool(name="square_pool", bufs=2))
+        stat_pool = ctx.enter_context(tc.tile_pool(name="stat_pool", bufs=5))
+        h_pool = ctx.enter_context(tc.tile_pool(name="h_pool", bufs=3))
+        out_pool = ctx.enter_context(tc.tile_pool(name="out_pool", bufs=8))
+        psum_t = ctx.enter_context(tc.psum_pool(name="psum_t", bufs=4))
+        psum_o = ctx.enter_context(tc.psum_pool(name="psum_o", bufs=4))
+
+        x1_dram = attn1.rearrange("b (q j) h d -> (b q) j (h d)", j=TILES)
+        x2_dram = attn2.rearrange("b (q j) h d -> (b q) j (h d)", j=TILES)
+        out_dram = out.rearrange("b (q j) e -> (b q) j e", j=TILES)
+        wo_dram = Wo.rearrange("(g t p) n -> g p t n", t=PACK, p=P)
+
+        lam_in = consts.tile([P, 4, LAM_D], BF16)
+        for i, vec in enumerate((lambda_q1, lambda_q2, lambda_k1, lambda_k2)):
+            nc.scalar.dma_start(out=lam_in[:, i, :], in_=vec.partition_broadcast(P))
+
+        x1 = resident.tile([P, TILES, K], BF16)
+        x2 = resident.tile([P, TILES, K], BF16)
+        wo_raw = resident.tile([P, PASSES, PACK, E], BF16)
+
+        def load_tokens(first, count):
+            js = slice(first, first + count)
+            nc.sync.dma_start(out=x2[:, js, :], in_=x2_dram[:, js, :])
+            nc.sync.dma_start(out=x1[:, js, :], in_=x1_dram[:, js, :])
+
+        def load_wo(g):
+            nc.sync.dma_start(out=wo_raw[:, g], in_=wo_dram[g])
+
+        load_tokens(0, 1)
+        load_tokens(1, 1)
+        w_raw = consts.tile([P, 1], BF16)
+        b_raw = consts.tile([P, 1], BF16)
+        with nc.allow_non_contiguous_dma(reason="128 elements, one to a partition"):
+            nc.sync.dma_start(out=w_raw[:], in_=ln_w.rearrange("(d o) -> d o", o=1))
+            nc.sync.dma_start(out=b_raw[:], in_=ln_b.rearrange("(d o) -> d o", o=1))
+        load_tokens(2, 1)
+        load_wo(0)
+        load_tokens(3, 1)
+        load_tokens(4, 2)
+        load_wo(1)
+        for first in range(6, TILES, 2):
+            load_tokens(first, 2)
+
+        ident = consts.tile([P, P], F32)
+        make_identity(nc, ident[:])
+        eps = consts.tile([P, 1], F32)
+        nc.vector.memset(eps[:], EPS)
+
+        prod = consts.tile([P, 2, LAM_D], F32)
+        nc.vector.tensor_tensor(out=prod[:], in0=lam_in[:, 0:2, :], in1=lam_in[:, 2:4, :], op=ALU.mult)
+        dots = consts.tile([P, 2], F32)
+        nc.vector.reduce_sum(out=dots[:], in_=prod[:], axis=AX.X)
+        exps = consts.tile([P, 2], F32)
+        nc.scalar.activation(out=exps[:], in_=dots[:], func=ACT.Exp)
+        neg_lam = consts.tile([P, 1], F32)
+        nc.vector.scalar_tensor_tensor(
+            out=neg_lam[:], in0=exps[:, 1:2], scalar=-LAMBDA_INIT, in1=exps[:, 0:1],
+            op0=ALU.add, op1=ALU.subtract,
+        )
+
+        wo_codes = resident.tile([P, PASSES, E], U32, align_bytes=64)
+        wo_scales = resident.tile([P, PASSES, E], U8, align_bytes=64)
+        h_codes = resident.tile([P, TILES, PASSES, P], U32, align_bytes=64)
+        h_scales = resident.tile([P, TILES, PASSES, P], U8, align_bytes=64)
+
+        wo_groups = {}
+        diffs = {}
+        roots = {}
+        flips = {}
+        h_groups = {}
+        sums = {}
+
+        def piece_of_wo(i):
+            g = i // PIECES_PER_PASS
+            first = (i % PIECES_PER_PASS) * PIECE_COLS
+            return g, slice(first, first + PIECE_COLS)
+
+        def regroup_wo(i):
+            g, cols = piece_of_wo(i)
+            wo_grouped = wo_stage.tile([P, PIECE_COLS, PACK], BF16, name="wo_grouped", align_bytes=64)
+            nc.vector.tensor_copy(
+                out=wo_grouped[:].rearrange("p (c i) t -> p c t i", i=4),
+                in_=wo_raw[:, g, :, cols].rearrange("p t (c i) -> p c t i", i=4),
+            )
+            wo_groups[i] = wo_grouped
+
+        def quantise_wo(i):
+            g, cols = piece_of_wo(i)
+            nc.vector.quantize_mx(
+                out=wo_codes[:, g, cols].bitcast(FP8X4),
+                scales=wo_scales[:, g, cols],
+                in_=wo_groups[i][:].rearrange("p n t -> p (n t)"),
+            )
+
+        def difference(j):
+            a = diff_pool.tile([P, K], F32, name="a")
+            nc.vector.scalar_tensor_tensor(
+                out=a[:], in0=x2[:, j, :], scalar=neg_lam[:, 0:1], in1=x1[:, j, :],
+                op0=ALU.mult, op1=ALU.add,
+            )
+            diffs[j] = a
+
+        def root_mean_square(j):
+            squares = square_pool.tile([P, K], BF16, name="squares")
+            ssq = stat_pool.tile([P, HEADS], F32, name="ssq")
+            for h in range(HEADS):
+                cols = slice(h * TD, (h + 1) * TD)
+                nc.scalar.activation(
+                    out=squares[:, cols], in_=diffs[j][:, cols], func=ACT.Square,
+                    accum_out=ssq[:, h : h + 1],
+                )
+            root = stat_pool.tile([P, HEADS], F32, name="root")
+            nc.scalar.activation(out=root[:], in_=ssq[:], func=ACT.Sqrt, scale=1.0 / TD, bias=eps[:, 0:1])
+            roots[j] = root
+
+        def normalise(j):
+            a = diffs[j]
+            rms = stat_pool.tile([P, HEADS], F32, name="rms")
+            nc.vector.reciprocal(out=rms[:], in_=roots[j][:])
+            for h in range(HEADS):
+                cols = slice(h * TD, (h + 1) * TD)
+                nc.vector.tensor_scalar_mul(out=a[:, cols], in0=a[:, cols], scalar1=rms[:, h : h + 1])
+
+        def transpose(j):
+            flips[j] = []
+            for g in range(PASSES):
+                flipped = psum_t.tile([P, HEADS_PER_PASS, P], F32, name="flipped")
+                for t in range(HEADS_PER_PASS):
+                    h = g * HEADS_PER_PASS + t
+                    nc.tensor.transpose(flipped[:, t, :], diffs[j][:, h * TD : (h + 1) * TD], ident[:])
+                flips[j].append(flipped)
+
+        def gain_and_bias(j):
+            h_grouped = h_pool.tile([P, PASSES, P, PACK], BF16, name="h_grouped", align_bytes=64)
+            for g in range(PASSES):
+                nc.scalar.activation(
+                    out=h_grouped[:, g], in_=flips[j][g][:].rearrange("p t r -> p r t"),
+                    func=ACT.Identity, scale=gain[:, 0:1], bias=shift[:, 0:1],
+                )
+            h_groups[j] = h_grouped
+
+        def quantise(j):
+            nc.vector.quantize_mx(
+                out=h_codes[:, j].rearrange("p g r -> p (g r)").bitcast(FP8X4),
+                scales=h_scales[:, j].rearrange("p g r -> p (g r)"),
+                in_=h_groups[j][:].rearrange("p g r t -> p (g r t)"),
+            )
+
+        def project(j):
+            for n in range(N_BANKS):
+                cols = slice(n * N_COLS, (n + 1) * N_COLS)
+                acc = psum_o.tile([P, N_COLS], F32, name="acc")
+                for g in range(PASSES):
+                    nc.tensor.matmul_mx(
+                        out=acc[:],
+                        lhsT=h_codes[:, j, g, :].bitcast(FP8X4),
+                        lhsT_scale=h_scales[:, j, g, :],
+                        rhs=wo_codes[:, g, cols].bitcast(FP8X4),
+                        rhs_scale=wo_scales[:, g, cols],
+                        start=(g == 0),
+                        stop=(g == PASSES - 1),
+                    )
+                sums[(j, n)] = acc
+
+        def store(j, n, on_scalar):
+            result = out_pool.tile([P, N_COLS], F32, name="result")
+            if on_scalar:
+                nc.scalar.copy(out=result[:], in_=sums[(j, n)][:])
+            else:
+                nc.vector.tensor_copy(out=result[:], in_=sums[(j, n)][:])
+            nc.sync.dma_start(out=out_dram[:, j, n * N_COLS : (n + 1) * N_COLS], in_=result[:])
+
+        difference(0)
+        difference(1)
+        root_mean_square(0)
+        difference(2)
+        root_mean_square(1)
+        normalise(0)
+        transpose(0)
+
+        gain = consts.tile([P, 1], F32)
+        shift = consts.tile([P, 1], F32)
+        nc.vector.tensor_scalar_mul(out=gain[:], in0=w_raw[:], scalar1=1.0 - LAMBDA_INIT)
+        nc.vector.tensor_scalar_mul(out=shift[:], in0=b_raw[:], scalar1=1.0 - LAMBDA_INIT)
+
+        for step in range(TILES):
+            if step < WO_PIECES:
+                tiles_to_project = []
+            else:
+                first = (step - WO_PIECES) * PROJECTIONS_A_STEP
+                tiles_to_project = list(range(first, first + PROJECTIONS_A_STEP))
+            gain_and_bias(step)
+            for j in tiles_to_project[:1]:
+                project(j)
+            if step + 1 < TILES:
+                normalise(step + 1)
+                transpose(step + 1)
+            if step < WO_PIECES:
+                regroup_wo(step)
+            if step + 3 < TILES:
+                difference(step + 3)
+            if step + 2 < TILES:
+                root_mean_square(step + 2)
+            quantise(step)
+            if step < WO_PIECES:
+                quantise_wo(step)
+            for j in tiles_to_project[1:]:
+                project(j)
+            for j in tiles_to_project:
+                for n in range(N_BANKS):
+                    store(j, n, on_scalar=(j == tiles_to_project[0] and n == 0))

@@ -42,6 +42,7 @@ def tile_multiheadflashdiff_pb_kernel(
 ):
     nc = tc.nc
     with ExitStack() as ctx:
+        ctx.enter_context(tc.manual_schedule())
         consts = ctx.enter_context(tc.tile_pool(name="consts", bufs=1))
         resident = ctx.enter_context(tc.tile_pool(name="resident", bufs=1))
         wo_stage = ctx.enter_context(tc.tile_pool(name="wo_stage", bufs=2))

@@ -42,7 +42,6 @@ def tile_multiheadflashdiff_pb_kernel(
 ):
     nc = tc.nc
     with ExitStack() as ctx:
-        ctx.enter_context(tc.manual_schedule())
         consts = ctx.enter_context(tc.tile_pool(name="consts", bufs=1))
         resident = ctx.enter_context(tc.tile_pool(name="resident", bufs=1))
         wo_stage = ctx.enter_context(tc.tile_pool(name="wo_stage", bufs=2))
@@ -61,7 +60,7 @@ def tile_multiheadflashdiff_pb_kernel(
 
         lam_in = consts.tile([P, 4, LAM_D], BF16)
         for i, vec in enumerate((lambda_q1, lambda_q2, lambda_k1, lambda_k2)):
-            nc.scalar.dma_start(out=lam_in[:, i, :], in_=vec.partition_broadcast(P))
+            nc.sync.dma_start(out=lam_in[:, i, :], in_=vec.partition_broadcast(P))
 
         x1 = resident.tile([P, TILES, K], BF16)
         x2 = resident.tile([P, TILES, K], BF16)
@@ -257,4 +256,4 @@ def tile_multiheadflashdiff_pb_kernel(
                 project(j)
             for j in tiles_to_project:
                 for n in range(N_BANKS):
-                    store(j, n, on_scalar=(j == tiles_to_project[0] and n == 0))
+                    store(j, n, on_scalar=(n == 0 and j % 4 != 1))

@@ -114,6 +114,7 @@ def tile_multiheadflashdiff_pb_kernel(
         wo_groups = {}
         diffs = {}
         roots = {}
+        scales = {}
         flips = {}
         h_groups = {}
         sums = {}
@@ -161,10 +162,14 @@ def tile_multiheadflashdiff_pb_kernel(
             nc.scalar.activation(out=root[:], in_=ssq[:], func=ACT.Sqrt, scale=1.0 / TD, bias=eps[:, 0:1])
             roots[j] = root
 
-        def normalise(j):
-            a = diffs[j]
+        def reciprocal(j):
             rms = stat_pool.tile([P, HEADS], F32, name="rms")
             nc.vector.reciprocal(out=rms[:], in_=roots[j][:])
+            scales[j] = rms
+
+        def normalise(j):
+            a = diffs[j]
+            rms = scales[j]
             for h in range(HEADS):
                 cols = slice(h * TD, (h + 1) * TD)
                 nc.vector.tensor_scalar_mul(out=a[:, cols], in0=a[:, cols], scalar1=rms[:, h : h + 1])
@@ -223,6 +228,7 @@ def tile_multiheadflashdiff_pb_kernel(
         root_mean_square(0)
         difference(2)
         root_mean_square(1)
+        reciprocal(0)
         normalise(0)
         transpose(0)
 
@@ -241,12 +247,14 @@ def tile_multiheadflashdiff_pb_kernel(
             for j in tiles_to_project[:1]:
                 project(j)
             if step + 1 < TILES:
+                reciprocal(step + 1)
+            if step + 3 < TILES:
+                difference(step + 3)
+            if step + 1 < TILES:
                 normalise(step + 1)
                 transpose(step + 1)
             if step < WO_PIECES:
                 regroup_wo(step)
-            if step + 3 < TILES:
-                difference(step + 3)
             if step + 2 < TILES:
                 root_mean_square(step + 2)
             quantise(step)

@@ -100,6 +100,8 @@ def tile_multiheadflashdiff_pb_kernel(
         nc.vector.reduce_sum(out=dots[:], in_=prod[:], axis=AX.X)
         exps = consts.tile([P, 2], F32)
         nc.scalar.activation(out=exps[:], in_=dots[:], func=ACT.Exp)
+        warm = consts.tile([P, 1], F32)
+        nc.scalar.activation(out=warm[:], in_=exps[:, 0:1], func=ACT.Abs_reciprocal_sqrt)
         neg_lam = consts.tile([P, 1], F32)
         nc.vector.scalar_tensor_tensor(
             out=neg_lam[:], in0=exps[:, 1:2], scalar=-LAMBDA_INIT, in1=exps[:, 0:1],
@@ -113,7 +115,6 @@ def tile_multiheadflashdiff_pb_kernel(
 
         wo_groups = {}
         diffs = {}
-        roots = {}
         scales = {}
         flips = {}
         h_groups = {}
@@ -158,13 +159,10 @@ def tile_multiheadflashdiff_pb_kernel(
                     out=squares[:, cols], in_=diffs[j][:, cols], func=ACT.Square,
                     accum_out=ssq[:, h : h + 1],
                 )
-            root = stat_pool.tile([P, HEADS], F32, name="root")
-            nc.scalar.activation(out=root[:], in_=ssq[:], func=ACT.Sqrt, scale=1.0 / TD, bias=eps[:, 0:1])
-            roots[j] = root
-
-        def reciprocal(j):
             rms = stat_pool.tile([P, HEADS], F32, name="rms")
-            nc.vector.reciprocal(out=rms[:], in_=roots[j][:])
+            nc.scalar.activation(
+                out=rms[:], in_=ssq[:], func=ACT.Abs_reciprocal_sqrt, scale=1.0 / TD, bias=eps[:, 0:1]
+            )
             scales[j] = rms
 
         def normalise(j):
@@ -228,7 +226,6 @@ def tile_multiheadflashdiff_pb_kernel(
         root_mean_square(0)
         difference(2)
         root_mean_square(1)
-        reciprocal(0)
         normalise(0)
         transpose(0)
 
@@ -246,8 +243,6 @@ def tile_multiheadflashdiff_pb_kernel(
             gain_and_bias(step)
             for j in tiles_to_project[:1]:
                 project(j)
-            if step + 1 < TILES:
-                reciprocal(step + 1)
             if step + 3 < TILES:
                 difference(step + 3)
             if step + 1 < TILES:

@@ -59,8 +59,11 @@ def tile_multiheadflashdiff_pb_kernel(
         wo_dram = Wo.rearrange("(g t p) n -> g p t n", t=PACK, p=P)
 
         lam_in = consts.tile([P, 4, LAM_D], BF16)
+        nc.vector.memset(lam_in[:], 0.0)
         for i, vec in enumerate((lambda_q1, lambda_q2, lambda_k1, lambda_k2)):
-            nc.sync.dma_start(out=lam_in[:, i, :], in_=vec.partition_broadcast(P))
+            nc.sync.dma_start(out=lam_in[0:1, i, :], in_=vec.rearrange("(o d) -> o d", o=1))
+        ones = consts.tile([P, P], F32)
+        nc.vector.memset(ones[:], 1.0)
 
         x1 = resident.tile([P, TILES, K], BF16)
         x2 = resident.tile([P, TILES, K], BF16)
@@ -98,8 +101,10 @@ def tile_multiheadflashdiff_pb_kernel(
         nc.vector.tensor_tensor(out=prod[:], in0=lam_in[:, 0:2, :], in1=lam_in[:, 2:4, :], op=ALU.mult)
         dots = consts.tile([P, 2], F32)
         nc.vector.reduce_sum(out=dots[:], in_=prod[:], axis=AX.X)
+        spread = psum_o.tile([P, 2], F32, name="acc")
+        nc.tensor.matmul(spread[:], lhsT=ones[:], rhs=dots[:], start=True, stop=True)
         exps = consts.tile([P, 2], F32)
-        nc.scalar.activation(out=exps[:], in_=dots[:], func=ACT.Exp)
+        nc.scalar.activation(out=exps[:], in_=spread[:], func=ACT.Exp)
         warm = consts.tile([P, 1], F32)
         nc.scalar.activation(out=warm[:], in_=exps[:, 0:1], func=ACT.Abs_reciprocal_sqrt)
         neg_lam = consts.tile([P, 1], F32)

@@ -11,7 +11,6 @@ U8 = mybir.dt.uint8
 FP8X4 = mybir.dt.float8_e4m3fn_x4
 ALU = mybir.AluOpType
 ACT = mybir.ActivationFunctionType
-AX = mybir.AxisListType
 
 P = 128
 TOKENS = 4 * 512
@@ -27,10 +26,10 @@ HEADS_PER_PASS = K_PASS // TD
 N_COLS = 512
 N_BANKS = E // N_COLS
 TILES = TOKENS // P
-WO_PIECES = 8
-PIECES_PER_PASS = WO_PIECES // PASSES
-PIECE_COLS = E // PIECES_PER_PASS
-PROJECTIONS_A_STEP = TILES // (TILES - WO_PIECES)
+PIECE_COLS = 256
+PIECES_PER_PASS = N_COLS // PIECE_COLS
+PIECES_PER_BANK = PASSES * PIECES_PER_PASS
+WO_PIECES = N_BANKS * PIECES_PER_BANK
 LAMBDA_INIT = 0.8 - 0.6 * math.exp(-0.3 * 12)
 EPS = 1e-8
 
@@ -56,26 +55,28 @@ def tile_multiheadflashdiff_pb_kernel(
         x1_dram = attn1.rearrange("b (q j) h d -> (b q) j (h d)", j=TILES)
         x2_dram = attn2.rearrange("b (q j) h d -> (b q) j (h d)", j=TILES)
         out_dram = out.rearrange("b (q j) e -> (b q) j e", j=TILES)
-        wo_dram = Wo.rearrange("(g t p) n -> g p t n", t=PACK, p=P)
+        wo_dram = Wo.rearrange("(g t p) n -> p (g t) n", t=PACK, p=P)
 
-        lam_in = consts.tile([P, 4, LAM_D], BF16)
-        nc.vector.memset(lam_in[:], 0.0)
-        for i, vec in enumerate((lambda_q1, lambda_q2, lambda_k1, lambda_k2)):
-            nc.sync.dma_start(out=lam_in[0:1, i, :], in_=vec.rearrange("(o d) -> o d", o=1))
+        lam_in = consts.tile([1, 4, LAM_D], BF16)
+        for i, vec in enumerate((lambda_q1, lambda_k1, lambda_q2, lambda_k2)):
+            nc.sync.dma_start(out=lam_in[:, i, :], in_=vec.rearrange("(o d) -> o d", o=1))
         ones = consts.tile([P, P], F32)
         nc.vector.memset(ones[:], 1.0)
+        dots = consts.tile([P, 2], F32)
+        nc.vector.memset(dots[:], 0.0)
 
         x1 = resident.tile([P, TILES, K], BF16)
         x2 = resident.tile([P, TILES, K], BF16)
-        wo_raw = resident.tile([P, PASSES, PACK, E], BF16)
+        wo_raw = resident.tile([P, PASSES * PACK, E], BF16)
 
         def load_tokens(first, count):
             js = slice(first, first + count)
             nc.sync.dma_start(out=x2[:, js, :], in_=x2_dram[:, js, :])
             nc.sync.dma_start(out=x1[:, js, :], in_=x1_dram[:, js, :])
 
-        def load_wo(g):
-            nc.sync.dma_start(out=wo_raw[:, g], in_=wo_dram[g])
+        def load_wo(n):
+            cols = slice(n * N_COLS, (n + 1) * N_COLS)
+            nc.sync.dma_start(out=wo_raw[:, :, cols], in_=wo_dram[:, :, cols])
 
         load_tokens(0, 1)
         load_tokens(1, 1)
@@ -97,10 +98,12 @@ def tile_multiheadflashdiff_pb_kernel(
         eps = consts.tile([P, 1], F32)
         nc.vector.memset(eps[:], EPS)
 
-        prod = consts.tile([P, 2, LAM_D], F32)
-        nc.vector.tensor_tensor(out=prod[:], in0=lam_in[:, 0:2, :], in1=lam_in[:, 2:4, :], op=ALU.mult)
-        dots = consts.tile([P, 2], F32)
-        nc.vector.reduce_sum(out=dots[:], in_=prod[:], axis=AX.X)
+        prod = consts.tile([1, 2, LAM_D], F32)
+        for i in range(2):
+            nc.vector.scalar_tensor_tensor(
+                out=prod[:, i, :], in0=lam_in[:, 2 * i, :], scalar=1.0, in1=lam_in[:, 2 * i + 1, :],
+                op0=ALU.mult, op1=ALU.mult, accum_out=dots[0:1, i : i + 1],
+            )
         spread = psum_o.tile([P, 2], F32, name="acc")
         nc.tensor.matmul(spread[:], lhsT=ones[:], rhs=dots[:], start=True, stop=True)
         exps = consts.tile([P, 2], F32)
@@ -126,8 +129,9 @@ def tile_multiheadflashdiff_pb_kernel(
         sums = {}
 
         def piece_of_wo(i):
-            g = i // PIECES_PER_PASS
-            first = (i % PIECES_PER_PASS) * PIECE_COLS
+            n, rest = divmod(i, PIECES_PER_BANK)
+            g, part = divmod(rest, PIECES_PER_PASS)
+            first = n * N_COLS + part * PIECE_COLS
             return g, slice(first, first + PIECE_COLS)
 
         def regroup_wo(i):
@@ -135,7 +139,7 @@ def tile_multiheadflashdiff_pb_kernel(
             wo_grouped = wo_stage.tile([P, PIECE_COLS, PACK], BF16, name="wo_grouped", align_bytes=64)
             nc.vector.tensor_copy(
                 out=wo_grouped[:].rearrange("p (c i) t -> p c t i", i=4),
-                in_=wo_raw[:, g, :, cols].rearrange("p t (c i) -> p c t i", i=4),
+                in_=wo_raw[:, g * PACK : (g + 1) * PACK, cols].rearrange("p t (c i) -> p c t i", i=4),
             )
             wo_groups[i] = wo_grouped
 
@@ -202,21 +206,20 @@ def tile_multiheadflashdiff_pb_kernel(
                 in_=h_groups[j][:].rearrange("p g r t -> p (g r t)"),
             )
 
-        def project(j):
-            for n in range(N_BANKS):
-                cols = slice(n * N_COLS, (n + 1) * N_COLS)
-                acc = psum_o.tile([P, N_COLS], F32, name="acc")
-                for g in range(PASSES):
-                    nc.tensor.matmul_mx(
-                        out=acc[:],
-                        lhsT=h_codes[:, j, g, :].bitcast(FP8X4),
-                        lhsT_scale=h_scales[:, j, g, :],
-                        rhs=wo_codes[:, g, cols].bitcast(FP8X4),
-                        rhs_scale=wo_scales[:, g, cols],
-                        start=(g == 0),
-                        stop=(g == PASSES - 1),
-                    )
-                sums[(j, n)] = acc
+        def project(j, n):
+            cols = slice(n * N_COLS, (n + 1) * N_COLS)
+            acc = psum_o.tile([P, N_COLS], F32, name="acc")
+            for g in range(PASSES):
+                nc.tensor.matmul_mx(
+                    out=acc[:],
+                    lhsT=h_codes[:, j, g, :].bitcast(FP8X4),
+                    lhsT_scale=h_scales[:, j, g, :],
+                    rhs=wo_codes[:, g, cols].bitcast(FP8X4),
+                    rhs_scale=wo_scales[:, g, cols],
+                    start=(g == 0),
+                    stop=(g == PASSES - 1),
+                )
+            sums[(j, n)] = acc
 
         def store(j, n, on_scalar):
             result = out_pool.tile([P, N_COLS], F32, name="result")
@@ -239,15 +242,20 @@ def tile_multiheadflashdiff_pb_kernel(
         nc.vector.tensor_scalar_mul(out=gain[:], in0=w_raw[:], scalar1=1.0 - LAMBDA_INIT)
         nc.vector.tensor_scalar_mul(out=shift[:], in0=b_raw[:], scalar1=1.0 - LAMBDA_INIT)
 
+        early = 6
+        banks = [(j, 0) for j in range(early)] + [(j, 1) for j in range(early)]
+        banks += [(j, n) for j in range(early, TILES) for n in range(N_BANKS)]
+        counts = {4: 1, 5: 2, 6: 1, 7: 2, 14: 4, 15: 4}
+        for step in range(8, 14):
+            counts[step] = 3
+
         for step in range(TILES):
-            if step < WO_PIECES:
-                tiles_to_project = []
-            else:
-                first = (step - WO_PIECES) * PROJECTIONS_A_STEP
-                tiles_to_project = list(range(first, first + PROJECTIONS_A_STEP))
+            count = counts.get(step, 0)
+            now, banks = banks[:count], banks[count:]
             gain_and_bias(step)
-            for j in tiles_to_project[:1]:
-                project(j)
+            for j, n in now:
+                if j < step:
+                    project(j, n)
             if step + 3 < TILES:
                 difference(step + 3)
             if step + 1 < TILES:
@@ -260,8 +268,13 @@ def tile_multiheadflashdiff_pb_kernel(
             quantise(step)
             if step < WO_PIECES:
                 quantise_wo(step)
-            for j in tiles_to_project[1:]:
-                project(j)
-            for j in tiles_to_project:
-                for n in range(N_BANKS):
-                    store(j, n, on_scalar=(n == 0 and j % 4 != 1))
+            for i, (j, n) in enumerate(now):
+                if j == step:
+                    project(j, n)
+                if step == TILES - 2:
+                    on_scalar = False
+                elif step == TILES - 1:
+                    on_scalar = i % 2 == 0
+                else:
+                    on_scalar = i == 0
+                store(j, n, on_scalar)

@@ -59,7 +59,7 @@ def tile_multiheadflashdiff_pb_kernel(
 
         lam_in = consts.tile([1, 4, LAM_D], BF16)
         for i, vec in enumerate((lambda_q1, lambda_k1, lambda_q2, lambda_k2)):
-            nc.sync.dma_start(out=lam_in[:, i, :], in_=vec.rearrange("(o d) -> o d", o=1))
+            nc.scalar.dma_start(out=lam_in[:, i, :], in_=vec.rearrange("(o d) -> o d", o=1))
         ones = consts.tile([P, P], F32)
         nc.vector.memset(ones[:], 1.0)
         dots = consts.tile([P, 2], F32)
@@ -78,7 +78,10 @@ def tile_multiheadflashdiff_pb_kernel(
             cols = slice(n * N_COLS, (n + 1) * N_COLS)
             nc.sync.dma_start(out=wo_raw[:, :, cols], in_=wo_dram[:, :, cols])
 
-        load_tokens(0, 1)
+        for n in range(N_BANKS):
+            cols = slice(n * N_COLS, (n + 1) * N_COLS)
+            nc.sync.dma_start(out=x2[:, 0, cols], in_=x2_dram[:, 0, cols])
+            nc.sync.dma_start(out=x1[:, 0, cols], in_=x1_dram[:, 0, cols])
         load_tokens(1, 1)
         w_raw = consts.tile([P, 1], BF16)
         b_raw = consts.tile([P, 1], BF16)
@@ -151,12 +154,15 @@ def tile_multiheadflashdiff_pb_kernel(
                 in_=wo_groups[i][:].rearrange("p n t -> p (n t)"),
             )
 
-        def difference(j):
+        def difference(j, parts=1):
             a = diff_pool.tile([P, K], F32, name="a")
-            nc.vector.scalar_tensor_tensor(
-                out=a[:], in0=x2[:, j, :], scalar=neg_lam[:, 0:1], in1=x1[:, j, :],
-                op0=ALU.mult, op1=ALU.add,
-            )
+            width = K // parts
+            for first in range(0, K, width):
+                cols = slice(first, first + width)
+                nc.vector.scalar_tensor_tensor(
+                    out=a[:, cols], in0=x2[:, j, cols], scalar=neg_lam[:, 0:1], in1=x1[:, j, cols],
+                    op0=ALU.mult, op1=ALU.add,
+                )
             diffs[j] = a
 
         def root_mean_square(j):
@@ -229,7 +235,7 @@ def tile_multiheadflashdiff_pb_kernel(
                 nc.vector.tensor_copy(out=result[:], in_=sums[(j, n)][:])
             nc.sync.dma_start(out=out_dram[:, j, n * N_COLS : (n + 1) * N_COLS], in_=result[:])
 
-        difference(0)
+        difference(0, parts=N_BANKS)
         difference(1)
         root_mean_square(0)
         difference(2)
@@ -253,14 +259,14 @@ def tile_multiheadflashdiff_pb_kernel(
             count = counts.get(step, 0)
             now, banks = banks[:count], banks[count:]
             gain_and_bias(step)
-            for j, n in now:
-                if j < step:
-                    project(j, n)
-            if step + 3 < TILES:
-                difference(step + 3)
             if step + 1 < TILES:
                 normalise(step + 1)
                 transpose(step + 1)
+            if step + 3 < TILES:
+                difference(step + 3)
+            for j, n in now:
+                if j < step:
+                    project(j, n)
             if step < WO_PIECES:
                 regroup_wo(step)
             if step + 2 < TILES:

@@ -59,7 +59,7 @@ def tile_multiheadflashdiff_pb_kernel(
 
         lam_in = consts.tile([1, 4, LAM_D], BF16)
         for i, vec in enumerate((lambda_q1, lambda_k1, lambda_q2, lambda_k2)):
-            nc.scalar.dma_start(out=lam_in[:, i, :], in_=vec.rearrange("(o d) -> o d", o=1))
+            nc.sync.dma_start(out=lam_in[:, i, :], in_=vec.rearrange("(o d) -> o d", o=1))
         ones = consts.tile([P, P], F32)
         nc.vector.memset(ones[:], 1.0)
         dots = consts.tile([P, 2], F32)
@@ -212,9 +212,8 @@ def tile_multiheadflashdiff_pb_kernel(
                 in_=h_groups[j][:].rearrange("p g r t -> p (g r t)"),
             )
 
-        def project(j, n):
-            cols = slice(n * N_COLS, (n + 1) * N_COLS)
-            acc = psum_o.tile([P, N_COLS], F32, name="acc")
+        def project(j, cols):
+            acc = psum_o.tile([P, cols.stop - cols.start], F32, name="acc")
             for g in range(PASSES):
                 nc.tensor.matmul_mx(
                     out=acc[:],
@@ -225,15 +224,16 @@ def tile_multiheadflashdiff_pb_kernel(
                     start=(g == 0),
                     stop=(g == PASSES - 1),
                 )
-            sums[(j, n)] = acc
+            sums[(j, cols.start)] = acc
 
-        def store(j, n, on_scalar):
-            result = out_pool.tile([P, N_COLS], F32, name="result")
+        def store(j, cols, on_scalar):
+            acc = sums[(j, cols.start)]
+            result = out_pool.tile([P, cols.stop - cols.start], F32, name="result")
             if on_scalar:
-                nc.scalar.copy(out=result[:], in_=sums[(j, n)][:])
+                nc.scalar.copy(out=result[:], in_=acc[:])
             else:
-                nc.vector.tensor_copy(out=result[:], in_=sums[(j, n)][:])
-            nc.sync.dma_start(out=out_dram[:, j, n * N_COLS : (n + 1) * N_COLS], in_=result[:])
+                nc.vector.tensor_copy(out=result[:], in_=acc[:])
+            nc.sync.dma_start(out=out_dram[:, j, cols], in_=result[:])
 
         difference(0, parts=N_BANKS)
         difference(1)
@@ -249,9 +249,12 @@ def tile_multiheadflashdiff_pb_kernel(
         nc.vector.tensor_scalar_mul(out=shift[:], in0=b_raw[:], scalar1=1.0 - LAMBDA_INIT)
 
         early = 6
-        banks = [(j, 0) for j in range(early)] + [(j, 1) for j in range(early)]
-        banks += [(j, n) for j in range(early, TILES) for n in range(N_BANKS)]
-        counts = {4: 1, 5: 2, 6: 1, 7: 2, 14: 4, 15: 4}
+        halves = [slice(n * N_COLS, (n + 1) * N_COLS) for n in range(N_BANKS)]
+        banks = [(j, cols) for cols in halves for j in range(early)]
+        banks += [(j, cols) for j in range(early, TILES) for cols in halves]
+        quarter = N_COLS // 2
+        banks[-1:] = [(TILES - 1, slice(first, first + quarter)) for first in range(E - N_COLS, E, quarter)]
+        counts = {4: 1, 5: 2, 6: 1, 7: 2, 14: 4, 15: 5}
         for step in range(8, 14):
             counts[step] = 3
 
@@ -264,9 +267,9 @@ def tile_multiheadflashdiff_pb_kernel(
                 transpose(step + 1)
             if step + 3 < TILES:
                 difference(step + 3)
-            for j, n in now:
+            for j, cols in now:
                 if j < step:
-                    project(j, n)
+                    project(j, cols)
             if step < WO_PIECES:
                 regroup_wo(step)
             if step + 2 < TILES:
@@ -274,13 +277,13 @@ def tile_multiheadflashdiff_pb_kernel(
             quantise(step)
             if step < WO_PIECES:
                 quantise_wo(step)
-            for i, (j, n) in enumerate(now):
+            for i, (j, cols) in enumerate(now):
                 if j == step:
-                    project(j, n)
+                    project(j, cols)
                 if step == TILES - 2:
                     on_scalar = False
                 elif step == TILES - 1:
                     on_scalar = i % 2 == 0
                 else:
                     on_scalar = i == 0
-                store(j, n, on_scalar)
+                store(j, cols, on_scalar)

@@ -78,16 +78,13 @@ def tile_multiheadflashdiff_pb_kernel(
             cols = slice(n * N_COLS, (n + 1) * N_COLS)
             nc.sync.dma_start(out=wo_raw[:, :, cols], in_=wo_dram[:, :, cols])
 
-        for n in range(N_BANKS):
-            cols = slice(n * N_COLS, (n + 1) * N_COLS)
-            nc.sync.dma_start(out=x2[:, 0, cols], in_=x2_dram[:, 0, cols])
-            nc.sync.dma_start(out=x1[:, 0, cols], in_=x1_dram[:, 0, cols])
+        load_tokens(0, 1)
         load_tokens(1, 1)
         w_raw = consts.tile([P, 1], BF16)
         b_raw = consts.tile([P, 1], BF16)
         with nc.allow_non_contiguous_dma(reason="128 elements, one to a partition"):
-            nc.sync.dma_start(out=w_raw[:], in_=ln_w.rearrange("(d o) -> d o", o=1))
-            nc.sync.dma_start(out=b_raw[:], in_=ln_b.rearrange("(d o) -> d o", o=1))
+            nc.gpsimd.dma_start(out=w_raw[:], in_=ln_w.rearrange("(d o) -> d o", o=1))
+            nc.gpsimd.dma_start(out=b_raw[:], in_=ln_b.rearrange("(d o) -> d o", o=1))
         load_tokens(2, 1)
         load_wo(0)
         load_tokens(3, 1)

@@ -83,8 +83,8 @@ def tile_multiheadflashdiff_pb_kernel(
         w_raw = consts.tile([P, 1], BF16)
         b_raw = consts.tile([P, 1], BF16)
         with nc.allow_non_contiguous_dma(reason="128 elements, one to a partition"):
-            nc.gpsimd.dma_start(out=w_raw[:], in_=ln_w.rearrange("(d o) -> d o", o=1))
-            nc.gpsimd.dma_start(out=b_raw[:], in_=ln_b.rearrange("(d o) -> d o", o=1))
+            nc.sync.dma_start(out=w_raw[:], in_=ln_w.rearrange("(d o) -> d o", o=1))
+            nc.sync.dma_start(out=b_raw[:], in_=ln_b.rearrange("(d o) -> d o", o=1))
         load_tokens(2, 1)
         load_wo(0)
         load_tokens(3, 1)

@@ -57,13 +57,14 @@ def tile_multiheadflashdiff_pb_kernel(
         out_dram = out.rearrange("b (q j) e -> (b q) j e", j=TILES)
         wo_dram = Wo.rearrange("(g t p) n -> p (g t) n", t=PACK, p=P)
 
-        lam_in = consts.tile([1, 4, LAM_D], BF16)
-        for i, vec in enumerate((lambda_q1, lambda_k1, lambda_q2, lambda_k2)):
-            nc.sync.dma_start(out=lam_in[:, i, :], in_=vec.rearrange("(o d) -> o d", o=1))
-        ones = consts.tile([P, P], F32)
-        nc.vector.memset(ones[:], 1.0)
-        dots = consts.tile([P, 2], F32)
-        nc.vector.memset(dots[:], 0.0)
+        lam_in = []
+        for i in range(4):
+            column = consts.tile([P, 1], BF16, name="lam_" + str(i))
+            nc.gpsimd.memset(column[:], 0.0)
+            lam_in.append(column)
+        with nc.allow_non_contiguous_dma(reason="64 elements, one to a partition"):
+            for column, vec in zip(lam_in, (lambda_q1, lambda_k1, lambda_q2, lambda_k2)):
+                nc.sync.dma_start(out=column[0:LAM_D, :], in_=vec.rearrange("(d o) -> d o", o=1))
 
         x1 = resident.tile([P, TILES, K], BF16)
         x2 = resident.tile([P, TILES, K], BF16)
@@ -98,16 +99,14 @@ def tile_multiheadflashdiff_pb_kernel(
         eps = consts.tile([P, 1], F32)
         nc.vector.memset(eps[:], EPS)
 
-        prod = consts.tile([1, 2, LAM_D], F32)
+        dots = psum_o.tile([P, 2], F32, name="acc")
         for i in range(2):
-            nc.vector.scalar_tensor_tensor(
-                out=prod[:, i, :], in0=lam_in[:, 2 * i, :], scalar=1.0, in1=lam_in[:, 2 * i + 1, :],
-                op0=ALU.mult, op1=ALU.mult, accum_out=dots[0:1, i : i + 1],
+            nc.tensor.matmul(
+                dots[:, i : i + 1], lhsT=lam_in[2 * i][:].to_broadcast([P, P]), rhs=lam_in[2 * i + 1][:],
+                start=True, stop=True,
             )
-        spread = psum_o.tile([P, 2], F32, name="acc")
-        nc.tensor.matmul(spread[:], lhsT=ones[:], rhs=dots[:], start=True, stop=True)
         exps = consts.tile([P, 2], F32)
-        nc.scalar.activation(out=exps[:], in_=spread[:], func=ACT.Exp)
+        nc.scalar.activation(out=exps[:], in_=dots[:], func=ACT.Exp)
         warm = consts.tile([P, 1], F32)
         nc.scalar.activation(out=warm[:], in_=exps[:, 0:1], func=ACT.Abs_reciprocal_sqrt)
         neg_lam = consts.tile([P, 1], F32)

import math
from contextlib import ExitStack

import concourse.mybir as mybir
from concourse.masks import make_identity

F32 = mybir.dt.float32
BF16 = mybir.dt.bfloat16
U32 = mybir.dt.uint32
U8 = mybir.dt.uint8
FP8X4 = mybir.dt.float8_e4m3fn_x4
ALU = mybir.AluOpType
ACT = mybir.ActivationFunctionType

P = 128
TOKENS = 4 * 512
HEADS = 8
TD = 128
K = HEADS * TD
E = 1024
LAM_D = 64
PACK = 4
K_PASS = P * PACK
PASSES = K // K_PASS
HEADS_PER_PASS = K_PASS // TD
N_COLS = 512
N_BANKS = E // N_COLS
TILES = TOKENS // P
PIECE_COLS = 256
PIECES_PER_PASS = N_COLS // PIECE_COLS
PIECES_PER_BANK = PASSES * PIECES_PER_PASS
WO_PIECES = N_BANKS * PIECES_PER_BANK
LAMBDA_INIT = 0.8 - 0.6 * math.exp(-0.3 * 12)
EPS = 1e-8

FLOPS = 2 * TOKENS * K * E


def tile_multiheadflashdiff_pb_kernel(
    tc, attn1, attn2, lambda_q1, lambda_k1, lambda_q2, lambda_k2, ln_w, ln_b, Wo, out
):
    nc = tc.nc
    with ExitStack() as ctx:
        consts = ctx.enter_context(tc.tile_pool(name="consts", bufs=1))
        resident = ctx.enter_context(tc.tile_pool(name="resident", bufs=1))
        wo_stage = ctx.enter_context(tc.tile_pool(name="wo_stage", bufs=2))
        diff_pool = ctx.enter_context(tc.tile_pool(name="diff_pool", bufs=5))
        square_pool = ctx.enter_context(tc.tile_pool(name="square_pool", bufs=2))
        stat_pool = ctx.enter_context(tc.tile_pool(name="stat_pool", bufs=5))
        h_pool = ctx.enter_context(tc.tile_pool(name="h_pool", bufs=3))
        out_pool = ctx.enter_context(tc.tile_pool(name="out_pool", bufs=8))
        psum_t = ctx.enter_context(tc.psum_pool(name="psum_t", bufs=4))
        psum_o = ctx.enter_context(tc.psum_pool(name="psum_o", bufs=4))

        x1_dram = attn1.rearrange("b (q j) h d -> (b q) j (h d)", j=TILES)
        x2_dram = attn2.rearrange("b (q j) h d -> (b q) j (h d)", j=TILES)
        out_dram = out.rearrange("b (q j) e -> (b q) j e", j=TILES)
        wo_dram = Wo.rearrange("(g t p) n -> p (g t) n", t=PACK, p=P)

        lam_in = []
        for i in range(4):
            column = consts.tile([P, 1], BF16, name="lam_" + str(i))
            nc.gpsimd.memset(column[:], 0.0)
            lam_in.append(column)
        with nc.allow_non_contiguous_dma(reason="64 elements, one to a partition"):
            for column, vec in zip(lam_in, (lambda_q1, lambda_k1, lambda_q2, lambda_k2)):
                nc.sync.dma_start(out=column[0:LAM_D, :], in_=vec.rearrange("(d o) -> d o", o=1))

        x1 = resident.tile([P, TILES, K], BF16)
        x2 = resident.tile([P, TILES, K], BF16)
        wo_raw = resident.tile([P, PASSES * PACK, E], BF16)

        def load_tokens(first, count):
            js = slice(first, first + count)
            nc.sync.dma_start(out=x2[:, js, :], in_=x2_dram[:, js, :])
            nc.sync.dma_start(out=x1[:, js, :], in_=x1_dram[:, js, :])

        def load_wo(n):
            cols = slice(n * N_COLS, (n + 1) * N_COLS)
            nc.sync.dma_start(out=wo_raw[:, :, cols], in_=wo_dram[:, :, cols])

        load_tokens(0, 1)
        load_tokens(1, 1)
        w_raw = consts.tile([P, 1], BF16)
        b_raw = consts.tile([P, 1], BF16)
        with nc.allow_non_contiguous_dma(reason="128 elements, one to a partition"):
            nc.sync.dma_start(out=w_raw[:], in_=ln_w.rearrange("(d o) -> d o", o=1))
            nc.sync.dma_start(out=b_raw[:], in_=ln_b.rearrange("(d o) -> d o", o=1))
        load_tokens(2, 1)
        load_wo(0)
        load_tokens(3, 1)
        load_tokens(4, 2)
        load_wo(1)
        for first in range(6, TILES, 2):
            load_tokens(first, 2)

        ident = consts.tile([P, P], F32)
        make_identity(nc, ident[:])
        eps = consts.tile([P, 1], F32)
        nc.vector.memset(eps[:], EPS)

        dots = psum_o.tile([P, 2], F32, name="acc")
        for i in range(2):
            nc.tensor.matmul(
                dots[:, i : i + 1], lhsT=lam_in[2 * i][:].to_broadcast([P, P]), rhs=lam_in[2 * i + 1][:],
                start=True, stop=True,
            )
        exps = consts.tile([P, 2], F32)
        nc.scalar.activation(out=exps[:], in_=dots[:], func=ACT.Exp)
        warm = consts.tile([P, 1], F32)
        nc.scalar.activation(out=warm[:], in_=exps[:, 0:1], func=ACT.Abs_reciprocal_sqrt)
        neg_lam = consts.tile([P, 1], F32)
        nc.vector.scalar_tensor_tensor(
            out=neg_lam[:], in0=exps[:, 1:2], scalar=-LAMBDA_INIT, in1=exps[:, 0:1],
            op0=ALU.add, op1=ALU.subtract,
        )

        wo_codes = resident.tile([P, PASSES, E], U32, align_bytes=64)
        wo_scales = resident.tile([P, PASSES, E], U8, align_bytes=64)
        h_codes = resident.tile([P, TILES, PASSES, P], U32, align_bytes=64)
        h_scales = resident.tile([P, TILES, PASSES, P], U8, align_bytes=64)

        wo_groups = {}
        diffs = {}
        scales = {}
        flips = {}
        h_groups = {}
        sums = {}

        def piece_of_wo(i):
            n, rest = divmod(i, PIECES_PER_BANK)
            g, part = divmod(rest, PIECES_PER_PASS)
            first = n * N_COLS + part * PIECE_COLS
            return g, slice(first, first + PIECE_COLS)

        def regroup_wo(i):
            g, cols = piece_of_wo(i)
            wo_grouped = wo_stage.tile([P, PIECE_COLS, PACK], BF16, name="wo_grouped", align_bytes=64)
            nc.vector.tensor_copy(
                out=wo_grouped[:].rearrange("p (c i) t -> p c t i", i=4),
                in_=wo_raw[:, g * PACK : (g + 1) * PACK, cols].rearrange("p t (c i) -> p c t i", i=4),
            )
            wo_groups[i] = wo_grouped

        def quantise_wo(i):
            g, cols = piece_of_wo(i)
            nc.vector.quantize_mx(
                out=wo_codes[:, g, cols].bitcast(FP8X4),
                scales=wo_scales[:, g, cols],
                in_=wo_groups[i][:].rearrange("p n t -> p (n t)"),
            )

        def difference(j, parts=1):
            a = diff_pool.tile([P, K], F32, name="a")
            width = K // parts
            for first in range(0, K, width):
                cols = slice(first, first + width)
                nc.vector.scalar_tensor_tensor(
                    out=a[:, cols], in0=x2[:, j, cols], scalar=neg_lam[:, 0:1], in1=x1[:, j, cols],
                    op0=ALU.mult, op1=ALU.add,
                )
            diffs[j] = a

        def root_mean_square(j):
            squares = square_pool.tile([P, K], BF16, name="squares")
            ssq = stat_pool.tile([P, HEADS], F32, name="ssq")
            for h in range(HEADS):
                cols = slice(h * TD, (h + 1) * TD)
                nc.scalar.activation(
                    out=squares[:, cols], in_=diffs[j][:, cols], func=ACT.Square,
                    accum_out=ssq[:, h : h + 1],
                )
            rms = stat_pool.tile([P, HEADS], F32, name="rms")
            nc.scalar.activation(
                out=rms[:], in_=ssq[:], func=ACT.Abs_reciprocal_sqrt, scale=1.0 / TD, bias=eps[:, 0:1]
            )
            scales[j] = rms

        def normalise(j):
            a = diffs[j]
            rms = scales[j]
            for h in range(HEADS):
                cols = slice(h * TD, (h + 1) * TD)
                nc.vector.tensor_scalar_mul(out=a[:, cols], in0=a[:, cols], scalar1=rms[:, h : h + 1])

        def transpose(j):
            flips[j] = []
            for g in range(PASSES):
                flipped = psum_t.tile([P, HEADS_PER_PASS, P], F32, name="flipped")
                for t in range(HEADS_PER_PASS):
                    h = g * HEADS_PER_PASS + t
                    nc.tensor.transpose(flipped[:, t, :], diffs[j][:, h * TD : (h + 1) * TD], ident[:])
                flips[j].append(flipped)

        def gain_and_bias(j):
            h_grouped = h_pool.tile([P, PASSES, P, PACK], BF16, name="h_grouped", align_bytes=64)
            for g in range(PASSES):
                nc.scalar.activation(
                    out=h_grouped[:, g], in_=flips[j][g][:].rearrange("p t r -> p r t"),
                    func=ACT.Identity, scale=gain[:, 0:1], bias=shift[:, 0:1],
                )
            h_groups[j] = h_grouped

        def quantise(j):
            nc.vector.quantize_mx(
                out=h_codes[:, j].rearrange("p g r -> p (g r)").bitcast(FP8X4),
                scales=h_scales[:, j].rearrange("p g r -> p (g r)"),
                in_=h_groups[j][:].rearrange("p g r t -> p (g r t)"),
            )

        def project(j, cols):
            acc = psum_o.tile([P, cols.stop - cols.start], F32, name="acc")
            for g in range(PASSES):
                nc.tensor.matmul_mx(
                    out=acc[:],
                    lhsT=h_codes[:, j, g, :].bitcast(FP8X4),
                    lhsT_scale=h_scales[:, j, g, :],
                    rhs=wo_codes[:, g, cols].bitcast(FP8X4),
                    rhs_scale=wo_scales[:, g, cols],
                    start=(g == 0),
                    stop=(g == PASSES - 1),
                )
            sums[(j, cols.start)] = acc

        def store(j, cols, on_scalar):
            acc = sums[(j, cols.start)]
            result = out_pool.tile([P, cols.stop - cols.start], F32, name="result")
            if on_scalar:
                nc.scalar.copy(out=result[:], in_=acc[:])
            else:
                nc.vector.tensor_copy(out=result[:], in_=acc[:])
            nc.sync.dma_start(out=out_dram[:, j, cols], in_=result[:])

        difference(0, parts=N_BANKS)
        difference(1)
        root_mean_square(0)
        difference(2)
        root_mean_square(1)
        normalise(0)
        transpose(0)

        gain = consts.tile([P, 1], F32)
        shift = consts.tile([P, 1], F32)
        nc.vector.tensor_scalar_mul(out=gain[:], in0=w_raw[:], scalar1=1.0 - LAMBDA_INIT)
        nc.vector.tensor_scalar_mul(out=shift[:], in0=b_raw[:], scalar1=1.0 - LAMBDA_INIT)

        early = 6
        halves = [slice(n * N_COLS, (n + 1) * N_COLS) for n in range(N_BANKS)]
        banks = [(j, cols) for cols in halves for j in range(early)]
        banks += [(j, cols) for j in range(early, TILES) for cols in halves]
        quarter = N_COLS // 2
        banks[-1:] = [(TILES - 1, slice(first, first + quarter)) for first in range(E - N_COLS, E, quarter)]
        counts = {4: 1, 5: 2, 6: 1, 7: 2, 14: 4, 15: 5}
        for step in range(8, 14):
            counts[step] = 3

        for step in range(TILES):
            count = counts.get(step, 0)
            now, banks = banks[:count], banks[count:]
            gain_and_bias(step)
            if step + 1 < TILES:
                normalise(step + 1)
                transpose(step + 1)
            if step + 3 < TILES:
                difference(step + 3)
            for j, cols in now:
                if j < step:
                    project(j, cols)
            if step < WO_PIECES:
                regroup_wo(step)
            if step + 2 < TILES:
                root_mean_square(step + 2)
            quantise(step)
            if step < WO_PIECES:
                quantise_wo(step)
            for i, (j, cols) in enumerate(now):
                if j == step:
                    project(j, cols)
                if step == TILES - 2:
                    on_scalar = False
                elif step == TILES - 1:
                    on_scalar = i % 2 == 0
                else:
                    on_scalar = i == 0
                store(j, cols, on_scalar)
